import numpy as np
import ml_dtypes


def mxq(x, axis, fmt="e4m3"):
    dtype, down = {"e4m3": (ml_dtypes.float8_e4m3fn, 7), "e5m2": (ml_dtypes.float8_e5m2, 14)}[fmt]
    v = np.moveaxis(np.asarray(x, np.float32).astype(ml_dtypes.bfloat16).astype(np.float64), axis, -1)
    blocks = v.reshape(v.shape[:-1] + (-1, 32))
    amax = np.abs(blocks).max(-1, keepdims=True)
    byte = np.maximum(np.where(amax > 0, np.frexp(amax)[1] - 1 + 127, 0) - down, 1)
    scale = np.exp2(byte - 127.0)
    codes = (blocks / scale).astype(np.float32).astype(dtype).astype(np.float64)
    return np.moveaxis((codes * scale).reshape(v.shape), -1, axis)


WIDE = False


def mx_kscale(k):
    if not WIDE:
        return np.ones(k)
    levels = np.array([10, -10, 5, -5, 0])
    a = np.random.permutation(np.resize(levels, k // 512 * 4)).reshape(k // 512, 4)
    idx = np.arange(k)
    return np.exp2(a[idx // 512, idx % 128 // 32])


BF16 = ml_dtypes.bfloat16


def bf(x):
    return np.asarray(x, np.float32).astype(BF16)


def f64(x):
    return np.asarray(x).astype(np.float64)


B, C, H, W, DM, GH = 6, 1024, 16, 16, 128, 1024


def sigmoid(v):
    return 1.0 / (1.0 + np.exp(-v))


def setup_inputs():
    s = np.concatenate([mx_kscale(C), np.ones(C)])
    t = mx_kscale(GH)
    return {'x': bf(np.random.standard_normal((B, C, H, W)) * s[:C][None, :, None, None]),
            'agg': bf(np.random.standard_normal((B, C, H, W)) * 0.7),
            'g1w': bf(np.random.standard_normal((GH, 2 * C)) / np.sqrt(2 * C) * t[:, None] / s[None, :]),
            'g1b': bf(np.random.standard_normal(GH) * 0.3 * t),
            'g2w': bf(np.random.standard_normal((C, GH)) * 2.0 / np.sqrt(GH) / t[None, :]),
            'g2b': bf(np.random.standard_normal(C) * 0.3)}


def reference(x, agg, g1w, g1b, g2w, g2b):
    a = f64(agg).reshape(B, C, H * W)
    cat = np.concatenate([f64(x).reshape(B, C, H * W), a], axis=1)
    hidden = np.maximum((mxq(f64(g1w), 1, 'e4m3') @ mxq(cat, 1, 'e4m3')) + f64(g1b)[None, :, None], 0.0)
    gate = sigmoid((mxq(f64(g2w), 1, 'e4m3') @ mxq(hidden, 1, 'e4m3')) + f64(g2b)[None, :, None])
    return (a * gate).reshape(B, C, H, W)

@@ -1,0 +1,267 @@
+from contextlib import ExitStack
+
+import concourse.mybir as mybir
+from concourse.masks import make_identity
+
+F32 = mybir.dt.float32
+BF16 = mybir.dt.bfloat16
+U32 = mybir.dt.uint32
+U8 = mybir.dt.uint8
+FP8X4 = mybir.dt.float8_e4m3fn_x4
+ACT = mybir.ActivationFunctionType
+ALU = mybir.AluOpType
+
+P = 128
+PACK = 4
+IMAGES = 6
+CH = 1024
+PIX = 256
+HID = 1024
+PAIR = 2
+N_TILE = PAIR * PIX
+N_TILES = IMAGES // PAIR
+QUARTERS = 4
+C_PASSES = 2 * CH // (P * PACK)
+G_PASSES = HID // (P * PACK)
+RUN = 4
+
+FLOPS = 2 * IMAGES * PIX * (2 * CH * HID + HID * CH)
+
+
+def tile_graphaugmentation_pb_kernel(tc, x, agg, g1w, g1b, g2w, g2b, out):
+    nc = tc.nc
+
+    def by_quarters(images):
+        return images.rearrange(
+            "b (v p e) h w -> p b v e (h w)", v=QUARTERS, p=P, e=PAIR
+        )
+
+    x_rows = by_quarters(x)
+    agg_rows = by_quarters(agg)
+    out_rows = by_quarters(out)
+    g1w_rows = g1w.rearrange("(v p e) c -> p v e c", v=QUARTERS, p=P, e=PAIR)
+    g2w_rows = g2w.rearrange("(v p e) g -> p v e g", v=QUARTERS, p=P, e=PAIR)
+
+    with ExitStack() as ctx:
+        keep = ctx.enter_context(tc.tile_pool(name="keep", bufs=1))
+        cat_stage = ctx.enter_context(tc.tile_pool(name="cat_stage", bufs=3))
+        w_stage = ctx.enter_context(tc.tile_pool(name="w_stage", bufs=2))
+        hid_stage = ctx.enter_context(tc.tile_pool(name="hid_stage", bufs=2))
+        res_stage = ctx.enter_context(tc.tile_pool(name="res_stage", bufs=3))
+        t_psum = ctx.enter_context(tc.psum_pool(name="t_psum", bufs=4))
+        mm_psum = ctx.enter_context(tc.psum_pool(name="mm_psum", bufs=4))
+
+        ident = keep.tile([P, P], F32, name="ident")
+        make_identity(nc, ident[:])
+
+        zero = keep.tile([P, 1], F32, name="zero")
+        half = keep.tile([P, 1], F32, name="half")
+        nc.vector.memset(zero[:], 0.0)
+        nc.scalar.activation(out=half[:], in_=zero[:], func=ACT.Sigmoid)
+
+        b1_bf = keep.tile([P, QUARTERS, PAIR], BF16, name="b1_bf")
+        b2_bf = keep.tile([P, QUARTERS, PAIR], BF16, name="b2_bf")
+        nc.scalar.dma_start(
+            out=b1_bf[:], in_=g1b.rearrange("(v p e) -> p v e", v=QUARTERS, p=P, e=PAIR)
+        )
+        nc.scalar.dma_start(
+            out=b2_bf[:], in_=g2b.rearrange("(v p e) -> p v e", v=QUARTERS, p=P, e=PAIR)
+        )
+
+        x_raw = [
+            keep.tile([P, PAIR, QUARTERS * PAIR, PIX], BF16, name="x_raw%d" % j)
+            for j in range(N_TILES)
+        ]
+        agg_raw = [
+            keep.tile([P, PAIR, QUARTERS * PAIR, PIX], BF16, name="agg_raw%d" % j)
+            for j in range(N_TILES)
+        ]
+        w1_raw = [
+            keep.tile([P, PAIR, 2 * CH], BF16, name="w1_raw%d" % v) for v in range(QUARTERS)
+        ]
+        w2_raw = [
+            keep.tile([P, PAIR, HID], BF16, name="w2_raw%d" % v) for v in range(QUARTERS)
+        ]
+
+        def load_cat(j):
+            for raw, rows in ((x_raw[j], x_rows), (agg_raw[j], agg_rows)):
+                for i in range(PAIR):
+                    nc.sync.dma_start(
+                        out=raw[:, i].rearrange("p (v e) w -> p v e w", e=PAIR),
+                        in_=rows[:, PAIR * j + i],
+                    )
+
+        load_cat(0)
+        for v in range(QUARTERS):
+            nc.sync.dma_start(out=w1_raw[v][:], in_=g1w_rows[:, v])
+        for v in range(QUARTERS):
+            nc.sync.dma_start(out=w2_raw[v][:], in_=g2w_rows[:, v])
+        load_cat(1)
+        load_cat(2)
+
+        b1 = keep.tile([P, QUARTERS, PAIR], F32, name="b1")
+        b2 = keep.tile([P, QUARTERS, PAIR], F32, name="b2")
+        nc.vector.tensor_copy(out=b1[:], in_=b1_bf[:])
+        nc.vector.tensor_copy(out=b2[:], in_=b2_bf[:])
+
+        cat_codes = [
+            keep.tile([P, C_PASSES, N_TILE], U32, name="cat_codes%d" % j, align_bytes=64)
+            for j in range(N_TILES)
+        ]
+        cat_scales = [
+            keep.tile([P, C_PASSES, N_TILE], U8, name="cat_scales%d" % j, align_bytes=64)
+            for j in range(N_TILES)
+        ]
+        hid_codes = [
+            keep.tile([P, G_PASSES, N_TILE], U32, name="hid_codes%d" % j, align_bytes=64)
+            for j in range(N_TILES)
+        ]
+        hid_scales = [
+            keep.tile([P, G_PASSES, N_TILE], U8, name="hid_scales%d" % j, align_bytes=64)
+            for j in range(N_TILES)
+        ]
+        w1_codes = [
+            keep.tile([P, PAIR, C_PASSES, P], U32, name="w1_codes%d" % v, align_bytes=64)
+            for v in range(QUARTERS)
+        ]
+        w1_scales = [
+            keep.tile([P, PAIR, C_PASSES, P], U8, name="w1_scales%d" % v, align_bytes=64)
+            for v in range(QUARTERS)
+        ]
+        w2_codes = [
+            keep.tile([P, PAIR, G_PASSES, P], U32, name="w2_codes%d" % v, align_bytes=64)
+            for v in range(QUARTERS)
+        ]
+        w2_scales = [
+            keep.tile([P, PAIR, G_PASSES, P], U8, name="w2_scales%d" % v, align_bytes=64)
+            for v in range(QUARTERS)
+        ]
+
+        def regroup(grouped, rows):
+            nc.vector.tensor_copy(out=grouped, in_=rows)
+
+        def prepare_cat(j):
+            previous = None
+            for G in range(C_PASSES):
+                raw = x_raw[j] if G < C_PASSES // 2 else agg_raw[j]
+                first = PACK * (G % (C_PASSES // 2))
+                grouped = cat_stage.tile([P, N_TILE, PACK], BF16, name="cat_grouped", align_bytes=64)
+                regroup(
+                    grouped[:].rearrange("p (b c i) t -> p b c t i", b=PAIR, i=RUN),
+                    raw[:, :, first : first + PACK, :].rearrange("p b t (c i) -> p b c t i", i=RUN),
+                )
+                if previous is not None:
+                    quantise_cat(j, G - 1, previous)
+                previous = grouped
+            quantise_cat(j, C_PASSES - 1, previous)
+
+        def quantise_cat(j, G, grouped):
+            nc.vector.quantize_mx(
+                out=cat_codes[j][:, G, :].bitcast(FP8X4),
+                scales=cat_scales[j][:, G, :],
+                in_=grouped[:].rearrange("p n t -> p (n t)"),
+            )
+
+        def prepare_weights(raw, passes, codes, scales):
+            words = raw[:].bitcast(F32)
+            grouped = w_stage.tile([P, PAIR, passes, P, PACK], BF16, name="w_grouped", align_bytes=64)
+            grouped_words = grouped[:].bitcast(F32)
+            for e in range(PAIR):
+                for G0 in range(0, passes, 2):
+                    bank = t_psum.tile([P, 2, 2, P], F32, name="t_bank")
+                    for G in range(G0, G0 + 2):
+                        for u in range(2):
+                            first = P * (2 * G + u)
+                            nc.tensor.transpose(
+                                out=bank[:, G - G0, u, :],
+                                in_=words[:, e, first : first + P],
+                                identity=ident[:],
+                            )
+                    nc.scalar.copy(
+                        out=grouped_words[:, e, G0 : G0 + 2, :, :],
+                        in_=bank[:].rearrange("p g u m -> p g m u"),
+                    )
+            nc.vector.quantize_mx(
+                out=codes[:].rearrange("p e g m -> p (e g m)").bitcast(FP8X4),
+                scales=scales[:].rearrange("p e g m -> p (e g m)"),
+                in_=grouped[:].rearrange("p e g m t -> p (e g m t)"),
+            )
+
+        def product(w_codes, w_scales, e, passes, rhs_codes, rhs_scales):
+            acc = mm_psum.tile([P, N_TILE], F32, name="acc")
+            for G in range(passes):
+                nc.tensor.matmul_mx(
+                    out=acc[:],
+                    lhsT=w_codes[:, e, G, :].bitcast(FP8X4),
+                    lhsT_scale=w_scales[:, e, G, :],
+                    rhs=rhs_codes[:, G, :].bitcast(FP8X4),
+                    rhs_scale=rhs_scales[:, G, :],
+                    start=(G == 0),
+                    stop=(G == passes - 1),
+                )
+            return acc
+
+        def hidden_pass(j, G):
+            hid = hid_stage.tile([P, PACK, N_TILE], BF16, name="hid")
+            for u in range(2):
+                v = 2 * G + u
+                for e in range(PAIR):
+                    acc = product(w1_codes[v], w1_scales[v], e, C_PASSES, cat_codes[j], cat_scales[j])
+                    nc.scalar.activation(
+                        out=hid[:, 2 * u + e, :],
+                        in_=acc[:],
+                        func=ACT.Relu,
+                        bias=b1[:, v, e : e + 1],
+                        scale=1.0,
+                    )
+            return hid
+
+        def quantise_hidden(j, G, hid):
+            grouped = hid_stage.tile([P, N_TILE, PACK], BF16, name="hid_grouped", align_bytes=64)
+            regroup(
+                grouped[:].rearrange("p (c i) t -> p c t i", i=RUN),
+                hid[:].rearrange("p t (c i) -> p c t i", i=RUN),
+            )
+            nc.vector.quantize_mx(
+                out=hid_codes[j][:, G, :].bitcast(FP8X4),
+                scales=hid_scales[j][:, G, :],
+                in_=grouped[:].rearrange("p n t -> p (n t)"),
+            )
+
+        def gate_quarter(j, v):
+            res = res_stage.tile([P, PAIR, PAIR, PIX], F32, name="res")
+            for e in range(PAIR):
+                acc = product(w2_codes[v], w2_scales[v], e, G_PASSES, hid_codes[j], hid_scales[j])
+                nc.scalar.activation(
+                    out=res[:, :, e, :],
+                    in_=acc[:].rearrange("p (b w) -> p b w", b=PAIR),
+                    func=ACT.Sigmoid,
+                    bias=b2[:, v, e : e + 1],
+                    scale=1.0,
+                )
+            nc.vector.tensor_tensor(
+                out=res[:], in0=res[:], in1=agg_raw[j][:, :, PAIR * v : PAIR * v + PAIR, :], op=ALU.mult
+            )
+            nc.sync.dma_start(
+                out=out_rows[:, PAIR * j : PAIR * j + PAIR, v], in_=res[:]
+            )
+
+        prepare_cat(0)
+        for v in range(QUARTERS):
+            prepare_weights(w1_raw[v], C_PASSES, w1_codes[v], w1_scales[v])
+        for G in range(G_PASSES):
+            quantise_hidden(0, G, hidden_pass(0, G))
+        for v in range(QUARTERS):
+            prepare_weights(w2_raw[v], G_PASSES, w2_codes[v], w2_scales[v])
+        prepare_cat(1)
+        for v in range(QUARTERS):
+            gate_quarter(0, v)
+        for G in range(G_PASSES):
+            quantise_hidden(1, G, hidden_pass(1, G))
+        prepare_cat(2)
+        for G in range(G_PASSES):
+            quantise_hidden(2, G, hidden_pass(2, G))
+            for v in (2 * G, 2 * G + 1):
+                gate_quarter(1, v)
+        for v in range(QUARTERS):
+            gate_quarter(2, v)

@@ -47,9 +47,10 @@ def tile_graphaugmentation_pb_kernel(tc, x, agg, g1w, g1b, g2w, g2b, out):
         cat_stage = ctx.enter_context(tc.tile_pool(name="cat_stage", bufs=3))
         w_stage = ctx.enter_context(tc.tile_pool(name="w_stage", bufs=2))
         hid_stage = ctx.enter_context(tc.tile_pool(name="hid_stage", bufs=2))
-        res_stage = ctx.enter_context(tc.tile_pool(name="res_stage", bufs=3))
-        t_psum = ctx.enter_context(tc.psum_pool(name="t_psum", bufs=4))
-        mm_psum = ctx.enter_context(tc.psum_pool(name="mm_psum", bufs=4))
+        res_stage = ctx.enter_context(tc.tile_pool(name="res_stage", bufs=5))
+        x_stage = ctx.enter_context(tc.tile_pool(name="x_stage", bufs=2))
+        psum = ctx.enter_context(tc.psum_pool(name="psum", bufs=8))
+        ctx.enter_context(tc.manual_schedule())
 
         ident = keep.tile([P, P], F32, name="ident")
         make_identity(nc, ident[:])
@@ -68,10 +69,7 @@ def tile_graphaugmentation_pb_kernel(tc, x, agg, g1w, g1b, g2w, g2b, out):
             out=b2_bf[:], in_=g2b.rearrange("(v p e) -> p v e", v=QUARTERS, p=P, e=PAIR)
         )
 
-        x_raw = [
-            keep.tile([P, PAIR, QUARTERS * PAIR, PIX], BF16, name="x_raw%d" % j)
-            for j in range(N_TILES)
-        ]
+        x_raw = []
         agg_raw = [
             keep.tile([P, PAIR, QUARTERS * PAIR, PIX], BF16, name="agg_raw%d" % j)
             for j in range(N_TILES)
@@ -84,6 +82,7 @@ def tile_graphaugmentation_pb_kernel(tc, x, agg, g1w, g1b, g2w, g2b, out):
         ]
 
         def load_cat(j):
+            x_raw.append(x_stage.tile([P, PAIR, QUARTERS * PAIR, PIX], BF16, name="x_raw"))
             for raw, rows in ((x_raw[j], x_rows), (agg_raw[j], agg_rows)):
                 for i in range(PAIR):
                     nc.sync.dma_start(
@@ -94,15 +93,12 @@ def tile_graphaugmentation_pb_kernel(tc, x, agg, g1w, g1b, g2w, g2b, out):
         load_cat(0)
         for v in range(QUARTERS):
             nc.sync.dma_start(out=w1_raw[v][:], in_=g1w_rows[:, v])
+        load_cat(1)
         for v in range(QUARTERS):
             nc.sync.dma_start(out=w2_raw[v][:], in_=g2w_rows[:, v])
-        load_cat(1)
-        load_cat(2)
 
         b1 = keep.tile([P, QUARTERS, PAIR], F32, name="b1")
         b2 = keep.tile([P, QUARTERS, PAIR], F32, name="b2")
-        nc.vector.tensor_copy(out=b1[:], in_=b1_bf[:])
-        nc.vector.tensor_copy(out=b2[:], in_=b2_bf[:])
 
         cat_codes = [
             keep.tile([P, C_PASSES, N_TILE], U32, name="cat_codes%d" % j, align_bytes=64)
@@ -137,23 +133,23 @@ def tile_graphaugmentation_pb_kernel(tc, x, agg, g1w, g1b, g2w, g2b, out):
             for v in range(QUARTERS)
         ]
 
-        def regroup(grouped, rows):
-            nc.vector.tensor_copy(out=grouped, in_=rows)
-
-        def prepare_cat(j):
-            previous = None
-            for G in range(C_PASSES):
-                raw = x_raw[j] if G < C_PASSES // 2 else agg_raw[j]
-                first = PACK * (G % (C_PASSES // 2))
+        def prepare_cat_half(j, x_half):
+            raw = x_raw[j] if x_half else agg_raw[j]
+            passes = (0, 1) if x_half else (3, 2)
+            tiles = []
+            for G in passes:
+                first = PACK * (G % 2)
                 grouped = cat_stage.tile([P, N_TILE, PACK], BF16, name="cat_grouped", align_bytes=64)
-                regroup(
-                    grouped[:].rearrange("p (b c i) t -> p b c t i", b=PAIR, i=RUN),
-                    raw[:, :, first : first + PACK, :].rearrange("p b t (c i) -> p b c t i", i=RUN),
-                )
-                if previous is not None:
-                    quantise_cat(j, G - 1, previous)
-                previous = grouped
-            quantise_cat(j, C_PASSES - 1, previous)
+                dst = grouped[:].rearrange("p (b c i) t -> p b c t i", b=PAIR, i=RUN)
+                src = raw[:, :, first : first + PACK, :].rearrange("p b t (c i) -> p b c t i", i=RUN)
+                if G == C_PASSES - 1:
+                    for i in range(PAIR):
+                        nc.scalar.copy(out=dst[:, i], in_=src[:, i])
+                else:
+                    nc.vector.tensor_copy(out=dst, in_=src)
+                tiles.append(grouped)
+            for G, grouped in zip(passes, tiles):
+                quantise_cat(j, G, grouped)
 
         def quantise_cat(j, G, grouped):
             nc.vector.quantize_mx(
@@ -168,7 +164,7 @@ def tile_graphaugmentation_pb_kernel(tc, x, agg, g1w, g1b, g2w, g2b, out):
             grouped_words = grouped[:].bitcast(F32)
             for e in range(PAIR):
                 for G0 in range(0, passes, 2):
-                    bank = t_psum.tile([P, 2, 2, P], F32, name="t_bank")
+                    bank = psum.tile([P, 2, 2, P], F32, name="t_bank", tag="bank")
                     for G in range(G0, G0 + 2):
                         for u in range(2):
                             first = P * (2 * G + u)
@@ -177,7 +173,9 @@ def tile_graphaugmentation_pb_kernel(tc, x, agg, g1w, g1b, g2w, g2b, out):
                                 in_=words[:, e, first : first + P],
                                 identity=ident[:],
                             )
-                    nc.scalar.copy(
+                    bank_no = (e * passes + G0) // 2
+                    copy_out = nc.scalar.copy if bank_no % 2 == 0 else nc.vector.tensor_copy
+                    copy_out(
                         out=grouped_words[:, e, G0 : G0 + 2, :, :],
                         in_=bank[:].rearrange("p g u m -> p g m u"),
                     )
@@ -188,7 +186,7 @@ def tile_graphaugmentation_pb_kernel(tc, x, agg, g1w, g1b, g2w, g2b, out):
             )
 
         def product(w_codes, w_scales, e, passes, rhs_codes, rhs_scales):
-            acc = mm_psum.tile([P, N_TILE], F32, name="acc")
+            acc = psum.tile([P, N_TILE], F32, name="acc", tag="bank")
             for G in range(passes):
                 nc.tensor.matmul_mx(
                     out=acc[:],
@@ -201,26 +199,22 @@ def tile_graphaugmentation_pb_kernel(tc, x, agg, g1w, g1b, g2w, g2b, out):
                 )
             return acc
 
-        def hidden_pass(j, G):
-            hid = hid_stage.tile([P, PACK, N_TILE], BF16, name="hid")
-            for u in range(2):
-                v = 2 * G + u
-                for e in range(PAIR):
-                    acc = product(w1_codes[v], w1_scales[v], e, C_PASSES, cat_codes[j], cat_scales[j])
-                    nc.scalar.activation(
-                        out=hid[:, 2 * u + e, :],
-                        in_=acc[:],
-                        func=ACT.Relu,
-                        bias=b1[:, v, e : e + 1],
-                        scale=1.0,
-                    )
-            return hid
+        def hidden_quarter(j, v, hid):
+            for e in range(PAIR):
+                acc = product(w1_codes[v], w1_scales[v], e, C_PASSES, cat_codes[j], cat_scales[j])
+                nc.scalar.activation(
+                    out=hid[:, PAIR * (v % 2) + e, :],
+                    in_=acc[:],
+                    func=ACT.Relu,
+                    bias=b1[:, v, e : e + 1],
+                    scale=1.0,
+                )
 
         def quantise_hidden(j, G, hid):
             grouped = hid_stage.tile([P, N_TILE, PACK], BF16, name="hid_grouped", align_bytes=64)
-            regroup(
-                grouped[:].rearrange("p (c i) t -> p c t i", i=RUN),
-                hid[:].rearrange("p t (c i) -> p c t i", i=RUN),
+            nc.vector.tensor_copy(
+                out=grouped[:].rearrange("p (c i) t -> p c t i", i=RUN),
+                in_=hid[:].rearrange("p t (c i) -> p c t i", i=RUN),
             )
             nc.vector.quantize_mx(
                 out=hid_codes[j][:, G, :].bitcast(FP8X4),
@@ -228,7 +222,7 @@ def tile_graphaugmentation_pb_kernel(tc, x, agg, g1w, g1b, g2w, g2b, out):
                 in_=grouped[:].rearrange("p n t -> p (n t)"),
             )
 
-        def gate_quarter(j, v):
+        def gate_products(j, v):
             res = res_stage.tile([P, PAIR, PAIR, PIX], F32, name="res")
             for e in range(PAIR):
                 acc = product(w2_codes[v], w2_scales[v], e, G_PASSES, hid_codes[j], hid_scales[j])
@@ -239,29 +233,52 @@ def tile_graphaugmentation_pb_kernel(tc, x, agg, g1w, g1b, g2w, g2b, out):
                     bias=b2[:, v, e : e + 1],
                     scale=1.0,
                 )
+            return res
+
+        def gate_apply(j, v, res):
             nc.vector.tensor_tensor(
                 out=res[:], in0=res[:], in1=agg_raw[j][:, :, PAIR * v : PAIR * v + PAIR, :], op=ALU.mult
             )
-            nc.sync.dma_start(
-                out=out_rows[:, PAIR * j : PAIR * j + PAIR, v], in_=res[:]
-            )
+            nc.sync.dma_start(out=out_rows[:, PAIR * j : PAIR * j + PAIR, v], in_=res[:])
 
-        prepare_cat(0)
-        for v in range(QUARTERS):
+        def new_hid():
+            return hid_stage.tile([P, PACK, N_TILE], BF16, name="hid")
+
+        prepare_cat_half(0, True)
+        prepare_cat_half(0, False)
+        load_cat(2)
+        nc.vector.tensor_copy(out=b1[:], in_=b1_bf[:])
+        nc.vector.tensor_copy(out=b2[:], in_=b2_bf[:])
+        for v in range(2):
             prepare_weights(w1_raw[v], C_PASSES, w1_codes[v], w1_scales[v])
-        for G in range(G_PASSES):
-            quantise_hidden(0, G, hidden_pass(0, G))
+
+        hid = None
         for v in range(QUARTERS):
+            if v % 2 == 0:
+                hid = new_hid()
+            hidden_quarter(0, v, hid)
+            if v < 2:
+                prepare_weights(w1_raw[v + 2], C_PASSES, w1_codes[v + 2], w1_scales[v + 2])
+                prepare_cat_half(1, v == 0)
+            if v == 1:
+                quantise_hidden(0, 0, hid)
+        prepare_weights(w2_raw[0], G_PASSES, w2_codes[0], w2_scales[0])
+        quantise_hidden(0, 1, hid)
+        for v in range(1, QUARTERS):
             prepare_weights(w2_raw[v], G_PASSES, w2_codes[v], w2_scales[v])
-        prepare_cat(1)
+
+        for j in range(1, N_TILES):
+            for v in range(QUARTERS):
+                if v % 2 == 0:
+                    hid = new_hid()
+                hidden_quarter(j, v, hid)
+                res = gate_products(j - 1, v - 1) if v > 0 else None
+                if j + 1 < N_TILES and v < 2:
+                    prepare_cat_half(j + 1, v == 0)
+                if v % 2 == 1:
+                    quantise_hidden(j, v // 2, hid)
+                if v > 0:
+                    gate_apply(j - 1, v - 1, res)
+            gate_apply(j - 1, QUARTERS - 1, gate_products(j - 1, QUARTERS - 1))
         for v in range(QUARTERS):
-            gate_quarter(0, v)
-        for G in range(G_PASSES):
-            quantise_hidden(1, G, hidden_pass(1, G))
-        prepare_cat(2)
-        for G in range(G_PASSES):
-            quantise_hidden(2, G, hidden_pass(2, G))
-            for v in (2 * G, 2 * G + 1):
-                gate_quarter(1, v)
-        for v in range(QUARTERS):
-            gate_quarter(2, v)
+            gate_apply(N_TILES - 1, v, gate_products(N_TILES - 1, v))

@@ -45,7 +45,7 @@ def tile_graphaugmentation_pb_kernel(tc, x, agg, g1w, g1b, g2w, g2b, out):
     with ExitStack() as ctx:
         keep = ctx.enter_context(tc.tile_pool(name="keep", bufs=1))
         cat_stage = ctx.enter_context(tc.tile_pool(name="cat_stage", bufs=3))
-        w_stage = ctx.enter_context(tc.tile_pool(name="w_stage", bufs=2))
+        w_stage = ctx.enter_context(tc.tile_pool(name="w_stage", bufs=4))
         hid_stage = ctx.enter_context(tc.tile_pool(name="hid_stage", bufs=2))
         res_stage = ctx.enter_context(tc.tile_pool(name="res_stage", bufs=5))
         x_stage = ctx.enter_context(tc.tile_pool(name="x_stage", bufs=2))
@@ -92,7 +92,8 @@ def tile_graphaugmentation_pb_kernel(tc, x, agg, g1w, g1b, g2w, g2b, out):
 
         load_cat(0)
         for v in range(QUARTERS):
-            nc.sync.dma_start(out=w1_raw[v][:], in_=g1w_rows[:, v])
+            for e in range(PAIR):
+                nc.sync.dma_start(out=w1_raw[v][:, e], in_=g1w_rows[:, v, e])
         load_cat(1)
         for v in range(QUARTERS):
             nc.sync.dma_start(out=w2_raw[v][:], in_=g2w_rows[:, v])
@@ -158,11 +159,11 @@ def tile_graphaugmentation_pb_kernel(tc, x, agg, g1w, g1b, g2w, g2b, out):
                 in_=grouped[:].rearrange("p n t -> p (n t)"),
             )
 
-        def prepare_weights(raw, passes, codes, scales):
+        def prepare_weights(raw, rows, passes, codes, scales):
             words = raw[:].bitcast(F32)
-            grouped = w_stage.tile([P, PAIR, passes, P, PACK], BF16, name="w_grouped", align_bytes=64)
+            grouped = w_stage.tile([P, len(rows), passes, P, PACK], BF16, name="w_grouped", align_bytes=64)
             grouped_words = grouped[:].bitcast(F32)
-            for e in range(PAIR):
+            for i, e in enumerate(rows):
                 for G0 in range(0, passes, 2):
                     bank = psum.tile([P, 2, 2, P], F32, name="t_bank", tag="bank")
                     for G in range(G0, G0 + 2):
@@ -173,17 +174,23 @@ def tile_graphaugmentation_pb_kernel(tc, x, agg, g1w, g1b, g2w, g2b, out):
                                 in_=words[:, e, first : first + P],
                                 identity=ident[:],
                             )
-                    bank_no = (e * passes + G0) // 2
-                    copy_out = nc.scalar.copy if bank_no % 2 == 0 else nc.vector.tensor_copy
-                    copy_out(
-                        out=grouped_words[:, e, G0 : G0 + 2, :, :],
+                    nc.scalar.copy(
+                        out=grouped_words[:, i, G0 : G0 + 2, :, :],
                         in_=bank[:].rearrange("p g u m -> p g m u"),
                     )
+            these = slice(rows[0], rows[0] + len(rows))
             nc.vector.quantize_mx(
-                out=codes[:].rearrange("p e g m -> p (e g m)").bitcast(FP8X4),
-                scales=scales[:].rearrange("p e g m -> p (e g m)"),
+                out=codes[:, these].rearrange("p e g m -> p (e g m)").bitcast(FP8X4),
+                scales=scales[:, these].rearrange("p e g m -> p (e g m)"),
                 in_=grouped[:].rearrange("p e g m t -> p (e g m t)"),
             )
+
+        def prepare_w1(v):
+            for e in range(PAIR):
+                prepare_weights(w1_raw[v], (e,), C_PASSES, w1_codes[v], w1_scales[v])
+
+        def prepare_w2(v):
+            prepare_weights(w2_raw[v], (0, 1), G_PASSES, w2_codes[v], w2_scales[v])
 
         def product(w_codes, w_scales, e, passes, rhs_codes, rhs_scales):
             acc = psum.tile([P, N_TILE], F32, name="acc", tag="bank")
@@ -199,16 +206,15 @@ def tile_graphaugmentation_pb_kernel(tc, x, agg, g1w, g1b, g2w, g2b, out):
                 )
             return acc
 
-        def hidden_quarter(j, v, hid):
-            for e in range(PAIR):
-                acc = product(w1_codes[v], w1_scales[v], e, C_PASSES, cat_codes[j], cat_scales[j])
-                nc.scalar.activation(
-                    out=hid[:, PAIR * (v % 2) + e, :],
-                    in_=acc[:],
-                    func=ACT.Relu,
-                    bias=b1[:, v, e : e + 1],
-                    scale=1.0,
-                )
+        def hidden_unit(j, v, e, hid):
+            acc = product(w1_codes[v], w1_scales[v], e, C_PASSES, cat_codes[j], cat_scales[j])
+            nc.scalar.activation(
+                out=hid[:, PAIR * (v % 2) + e, :],
+                in_=acc[:],
+                func=ACT.Relu,
+                bias=b1[:, v, e : e + 1],
+                scale=1.0,
+            )
 
         def quantise_hidden(j, G, hid):
             grouped = hid_stage.tile([P, N_TILE, PACK], BF16, name="hid_grouped", align_bytes=64)
@@ -250,28 +256,31 @@ def tile_graphaugmentation_pb_kernel(tc, x, agg, g1w, g1b, g2w, g2b, out):
         nc.vector.tensor_copy(out=b1[:], in_=b1_bf[:])
         nc.vector.tensor_copy(out=b2[:], in_=b2_bf[:])
         for v in range(2):
-            prepare_weights(w1_raw[v], C_PASSES, w1_codes[v], w1_scales[v])
+            prepare_w1(v)
 
         hid = None
         for v in range(QUARTERS):
             if v % 2 == 0:
                 hid = new_hid()
-            hidden_quarter(0, v, hid)
-            if v < 2:
-                prepare_weights(w1_raw[v + 2], C_PASSES, w1_codes[v + 2], w1_scales[v + 2])
-                prepare_cat_half(1, v == 0)
+            for e in range(PAIR):
+                hidden_unit(0, v, e, hid)
+                if v == 0:
+                    prepare_w1(2 + e)
+                if v < 2 and e == 1:
+                    prepare_cat_half(1, v == 0)
             if v == 1:
                 quantise_hidden(0, 0, hid)
-        prepare_weights(w2_raw[0], G_PASSES, w2_codes[0], w2_scales[0])
+        prepare_w2(0)
         quantise_hidden(0, 1, hid)
         for v in range(1, QUARTERS):
-            prepare_weights(w2_raw[v], G_PASSES, w2_codes[v], w2_scales[v])
+            prepare_w2(v)
 
         for j in range(1, N_TILES):
             for v in range(QUARTERS):
                 if v % 2 == 0:
                     hid = new_hid()
-                hidden_quarter(j, v, hid)
+                for e in range(PAIR):
+                    hidden_unit(j, v, e, hid)
                 res = gate_products(j - 1, v - 1) if v > 0 else None
                 if j + 1 < N_TILES and v < 2:
                     prepare_cat_half(j + 1, v == 0)

@@ -13,16 +13,21 @@ ALU = mybir.AluOpType
 
 P = 128
 PACK = 4
+HALVES = 2
+ROWS = 2
+QUARTERS = 4
 IMAGES = 6
 CH = 1024
 PIX = 256
 HID = 1024
-PAIR = 2
-N_TILE = PAIR * PIX
-N_TILES = IMAGES // PAIR
-QUARTERS = 4
+TILE_IMAGES = 2
+N_TILE = TILE_IMAGES * PIX
+N_TILES = IMAGES // TILE_IMAGES
 C_PASSES = 2 * CH // (P * PACK)
+X_PASSES = C_PASSES // 2
 G_PASSES = HID // (P * PACK)
+BANK_PASSES = 2
+PSUM_BANKS = 8
 RUN = 4
 
 FLOPS = 2 * IMAGES * PIX * (2 * CH * HID + HID * CH)
@@ -32,15 +37,13 @@ def tile_graphaugmentation_pb_kernel(tc, x, agg, g1w, g1b, g2w, g2b, out):
     nc = tc.nc
 
     def by_quarters(images):
-        return images.rearrange(
-            "b (v p e) h w -> p b v e (h w)", v=QUARTERS, p=P, e=PAIR
-        )
+        return images.rearrange("b (v p e) h w -> p b v e (h w)", v=QUARTERS, p=P, e=ROWS)
 
     x_rows = by_quarters(x)
     agg_rows = by_quarters(agg)
     out_rows = by_quarters(out)
-    g1w_rows = g1w.rearrange("(v p e) c -> p v e c", v=QUARTERS, p=P, e=PAIR)
-    g2w_rows = g2w.rearrange("(v p e) g -> p v e g", v=QUARTERS, p=P, e=PAIR)
+    g1w_rows = g1w.rearrange("(v p e) c -> p v e c", v=QUARTERS, p=P, e=ROWS)
+    g2w_rows = g2w.rearrange("(v p e) g -> p v e g", v=QUARTERS, p=P, e=ROWS)
 
     with ExitStack() as ctx:
         keep = ctx.enter_context(tc.tile_pool(name="keep", bufs=1))
@@ -49,7 +52,7 @@ def tile_graphaugmentation_pb_kernel(tc, x, agg, g1w, g1b, g2w, g2b, out):
         hid_stage = ctx.enter_context(tc.tile_pool(name="hid_stage", bufs=2))
         res_stage = ctx.enter_context(tc.tile_pool(name="res_stage", bufs=5))
         x_stage = ctx.enter_context(tc.tile_pool(name="x_stage", bufs=2))
-        psum = ctx.enter_context(tc.psum_pool(name="psum", bufs=8))
+        psum = ctx.enter_context(tc.psum_pool(name="psum", bufs=PSUM_BANKS))
         ctx.enter_context(tc.manual_schedule())
 
         ident = keep.tile([P, P], F32, name="ident")
@@ -60,46 +63,42 @@ def tile_graphaugmentation_pb_kernel(tc, x, agg, g1w, g1b, g2w, g2b, out):
         nc.vector.memset(zero[:], 0.0)
         nc.scalar.activation(out=half[:], in_=zero[:], func=ACT.Sigmoid)
 
-        b1_bf = keep.tile([P, QUARTERS, PAIR], BF16, name="b1_bf")
-        b2_bf = keep.tile([P, QUARTERS, PAIR], BF16, name="b2_bf")
-        nc.scalar.dma_start(
-            out=b1_bf[:], in_=g1b.rearrange("(v p e) -> p v e", v=QUARTERS, p=P, e=PAIR)
-        )
-        nc.scalar.dma_start(
-            out=b2_bf[:], in_=g2b.rearrange("(v p e) -> p v e", v=QUARTERS, p=P, e=PAIR)
-        )
+        b1_bf = keep.tile([P, QUARTERS, ROWS], BF16, name="b1_bf")
+        b2_bf = keep.tile([P, QUARTERS, ROWS], BF16, name="b2_bf")
 
         x_raw = []
         agg_raw = [
-            keep.tile([P, PAIR, QUARTERS * PAIR, PIX], BF16, name="agg_raw%d" % j)
+            keep.tile([P, TILE_IMAGES, QUARTERS * ROWS, PIX], BF16, name="agg_raw%d" % j)
             for j in range(N_TILES)
         ]
-        w1_raw = [
-            keep.tile([P, PAIR, 2 * CH], BF16, name="w1_raw%d" % v) for v in range(QUARTERS)
-        ]
-        w2_raw = [
-            keep.tile([P, PAIR, HID], BF16, name="w2_raw%d" % v) for v in range(QUARTERS)
-        ]
+        w1_raw = [keep.tile([P, ROWS, 2 * CH], BF16, name="w1_raw%d" % v) for v in range(QUARTERS)]
+        w2_raw = [keep.tile([P, ROWS, HID], BF16, name="w2_raw%d" % v) for v in range(QUARTERS)]
 
         def load_cat(j):
-            x_raw.append(x_stage.tile([P, PAIR, QUARTERS * PAIR, PIX], BF16, name="x_raw"))
+            x_raw.append(x_stage.tile([P, TILE_IMAGES, QUARTERS * ROWS, PIX], BF16, name="x_raw"))
             for raw, rows in ((x_raw[j], x_rows), (agg_raw[j], agg_rows)):
-                for i in range(PAIR):
+                for b in range(TILE_IMAGES):
                     nc.sync.dma_start(
-                        out=raw[:, i].rearrange("p (v e) w -> p v e w", e=PAIR),
-                        in_=rows[:, PAIR * j + i],
+                        out=raw[:, b].rearrange("p (v e) w -> p v e w", e=ROWS),
+                        in_=rows[:, TILE_IMAGES * j + b],
                     )
 
+        first_quarters = QUARTERS // 2
         load_cat(0)
         for v in range(QUARTERS):
-            for e in range(PAIR):
+            if v == first_quarters:
+                for b_bf, b_dram in ((b1_bf, g1b), (b2_bf, g2b)):
+                    nc.sync.dma_start(
+                        out=b_bf[:], in_=b_dram.rearrange("(v p e) -> p v e", v=QUARTERS, p=P, e=ROWS)
+                    )
+            for e in range(ROWS):
                 nc.sync.dma_start(out=w1_raw[v][:, e], in_=g1w_rows[:, v, e])
         load_cat(1)
         for v in range(QUARTERS):
             nc.sync.dma_start(out=w2_raw[v][:], in_=g2w_rows[:, v])
 
-        b1 = keep.tile([P, QUARTERS, PAIR], F32, name="b1")
-        b2 = keep.tile([P, QUARTERS, PAIR], F32, name="b2")
+        b1 = keep.tile([P, QUARTERS, ROWS], F32, name="b1")
+        b2 = keep.tile([P, QUARTERS, ROWS], F32, name="b2")
 
         cat_codes = [
             keep.tile([P, C_PASSES, N_TILE], U32, name="cat_codes%d" % j, align_bytes=64)
@@ -118,19 +117,19 @@ def tile_graphaugmentation_pb_kernel(tc, x, agg, g1w, g1b, g2w, g2b, out):
             for j in range(N_TILES)
         ]
         w1_codes = [
-            keep.tile([P, PAIR, C_PASSES, P], U32, name="w1_codes%d" % v, align_bytes=64)
+            keep.tile([P, ROWS, C_PASSES, P], U32, name="w1_codes%d" % v, align_bytes=64)
             for v in range(QUARTERS)
         ]
         w1_scales = [
-            keep.tile([P, PAIR, C_PASSES, P], U8, name="w1_scales%d" % v, align_bytes=64)
+            keep.tile([P, ROWS, C_PASSES, P], U8, name="w1_scales%d" % v, align_bytes=64)
             for v in range(QUARTERS)
         ]
         w2_codes = [
-            keep.tile([P, PAIR, G_PASSES, P], U32, name="w2_codes%d" % v, align_bytes=64)
+            keep.tile([P, ROWS, G_PASSES, P], U32, name="w2_codes%d" % v, align_bytes=64)
             for v in range(QUARTERS)
         ]
         w2_scales = [
-            keep.tile([P, PAIR, G_PASSES, P], U8, name="w2_scales%d" % v, align_bytes=64)
+            keep.tile([P, ROWS, G_PASSES, P], U8, name="w2_scales%d" % v, align_bytes=64)
             for v in range(QUARTERS)
         ]
 
@@ -139,43 +138,40 @@ def tile_graphaugmentation_pb_kernel(tc, x, agg, g1w, g1b, g2w, g2b, out):
             passes = (0, 1) if x_half else (3, 2)
             tiles = []
             for G in passes:
-                first = PACK * (G % 2)
+                first = PACK * (G % X_PASSES)
                 grouped = cat_stage.tile([P, N_TILE, PACK], BF16, name="cat_grouped", align_bytes=64)
-                dst = grouped[:].rearrange("p (b c i) t -> p b c t i", b=PAIR, i=RUN)
+                dst = grouped[:].rearrange("p (b c i) t -> p b c t i", b=TILE_IMAGES, i=RUN)
                 src = raw[:, :, first : first + PACK, :].rearrange("p b t (c i) -> p b c t i", i=RUN)
                 if G == C_PASSES - 1:
-                    for i in range(PAIR):
-                        nc.scalar.copy(out=dst[:, i], in_=src[:, i])
+                    for b in range(TILE_IMAGES):
+                        nc.scalar.copy(out=dst[:, b], in_=src[:, b])
                 else:
                     nc.vector.tensor_copy(out=dst, in_=src)
                 tiles.append(grouped)
             for G, grouped in zip(passes, tiles):
-                quantise_cat(j, G, grouped)
-
-        def quantise_cat(j, G, grouped):
-            nc.vector.quantize_mx(
-                out=cat_codes[j][:, G, :].bitcast(FP8X4),
-                scales=cat_scales[j][:, G, :],
-                in_=grouped[:].rearrange("p n t -> p (n t)"),
-            )
+                nc.vector.quantize_mx(
+                    out=cat_codes[j][:, G, :].bitcast(FP8X4),
+                    scales=cat_scales[j][:, G, :],
+                    in_=grouped[:].rearrange("p n t -> p (n t)"),
+                )
 
         def prepare_weights(raw, rows, passes, codes, scales):
             words = raw[:].bitcast(F32)
             grouped = w_stage.tile([P, len(rows), passes, P, PACK], BF16, name="w_grouped", align_bytes=64)
             grouped_words = grouped[:].bitcast(F32)
             for i, e in enumerate(rows):
-                for G0 in range(0, passes, 2):
-                    bank = psum.tile([P, 2, 2, P], F32, name="t_bank", tag="bank")
-                    for G in range(G0, G0 + 2):
-                        for u in range(2):
-                            first = P * (2 * G + u)
+                for G0 in range(0, passes, BANK_PASSES):
+                    bank = psum.tile([P, BANK_PASSES, HALVES, P], F32, name="t_bank", tag="bank")
+                    for G in range(G0, G0 + BANK_PASSES):
+                        for u in range(HALVES):
+                            first = P * (HALVES * G + u)
                             nc.tensor.transpose(
                                 out=bank[:, G - G0, u, :],
                                 in_=words[:, e, first : first + P],
                                 identity=ident[:],
                             )
                     nc.scalar.copy(
-                        out=grouped_words[:, i, G0 : G0 + 2, :, :],
+                        out=grouped_words[:, i, G0 : G0 + BANK_PASSES, :, :],
                         in_=bank[:].rearrange("p g u m -> p g m u"),
                     )
             these = slice(rows[0], rows[0] + len(rows))
@@ -186,7 +182,7 @@ def tile_graphaugmentation_pb_kernel(tc, x, agg, g1w, g1b, g2w, g2b, out):
             )
 
         def prepare_w1(v):
-            for e in range(PAIR):
+            for e in range(ROWS):
                 prepare_weights(w1_raw[v], (e,), C_PASSES, w1_codes[v], w1_scales[v])
 
         def prepare_w2(v):
@@ -206,10 +202,13 @@ def tile_graphaugmentation_pb_kernel(tc, x, agg, g1w, g1b, g2w, g2b, out):
                 )
             return acc
 
+        def new_hid():
+            return hid_stage.tile([P, PACK, N_TILE], BF16, name="hid")
+
         def hidden_unit(j, v, e, hid):
             acc = product(w1_codes[v], w1_scales[v], e, C_PASSES, cat_codes[j], cat_scales[j])
             nc.scalar.activation(
-                out=hid[:, PAIR * (v % 2) + e, :],
+                out=hid[:, ROWS * (v % HALVES) + e, :],
                 in_=acc[:],
                 func=ACT.Relu,
                 bias=b1[:, v, e : e + 1],
@@ -229,12 +228,12 @@ def tile_graphaugmentation_pb_kernel(tc, x, agg, g1w, g1b, g2w, g2b, out):
             )
 
         def gate_products(j, v):
-            res = res_stage.tile([P, PAIR, PAIR, PIX], F32, name="res")
-            for e in range(PAIR):
+            res = res_stage.tile([P, TILE_IMAGES, ROWS, PIX], F32, name="res")
+            for e in range(ROWS):
                 acc = product(w2_codes[v], w2_scales[v], e, G_PASSES, hid_codes[j], hid_scales[j])
                 nc.scalar.activation(
                     out=res[:, :, e, :],
-                    in_=acc[:].rearrange("p (b w) -> p b w", b=PAIR),
+                    in_=acc[:].rearrange("p (b w) -> p b w", b=TILE_IMAGES),
                     func=ACT.Sigmoid,
                     bias=b2[:, v, e : e + 1],
                     scale=1.0,
@@ -243,31 +242,27 @@ def tile_graphaugmentation_pb_kernel(tc, x, agg, g1w, g1b, g2w, g2b, out):
 
         def gate_apply(j, v, res):
             nc.vector.tensor_tensor(
-                out=res[:], in0=res[:], in1=agg_raw[j][:, :, PAIR * v : PAIR * v + PAIR, :], op=ALU.mult
+                out=res[:], in0=res[:], in1=agg_raw[j][:, :, ROWS * v : ROWS * v + ROWS, :], op=ALU.mult
             )
-            nc.sync.dma_start(out=out_rows[:, PAIR * j : PAIR * j + PAIR, v], in_=res[:])
-
-        def new_hid():
-            return hid_stage.tile([P, PACK, N_TILE], BF16, name="hid")
+            nc.sync.dma_start(out=out_rows[:, TILE_IMAGES * j : TILE_IMAGES * j + TILE_IMAGES, v], in_=res[:])
 
         prepare_cat_half(0, True)
         prepare_cat_half(0, False)
         load_cat(2)
+        for v in range(first_quarters):
+            prepare_w1(v)
         nc.vector.tensor_copy(out=b1[:], in_=b1_bf[:])
         nc.vector.tensor_copy(out=b2[:], in_=b2_bf[:])
-        for v in range(2):
-            prepare_w1(v)
 
-        hid = None
         for v in range(QUARTERS):
-            if v % 2 == 0:
+            if v % HALVES == 0:
                 hid = new_hid()
-            for e in range(PAIR):
+            for e in range(ROWS):
                 hidden_unit(0, v, e, hid)
                 if v == 0:
-                    prepare_w1(2 + e)
-                if v < 2 and e == 1:
-                    prepare_cat_half(1, v == 0)
+                    prepare_w1(first_quarters + e)
+            if v < 2:
+                prepare_cat_half(1, v == 0)
             if v == 1:
                 quantise_hidden(0, 0, hid)
         prepare_w2(0)
@@ -277,15 +272,16 @@ def tile_graphaugmentation_pb_kernel(tc, x, agg, g1w, g1b, g2w, g2b, out):
 
         for j in range(1, N_TILES):
             for v in range(QUARTERS):
-                if v % 2 == 0:
+                if v % HALVES == 0:
                     hid = new_hid()
-                for e in range(PAIR):
+                for e in range(ROWS):
                     hidden_unit(j, v, e, hid)
-                res = gate_products(j - 1, v - 1) if v > 0 else None
+                if v > 0:
+                    res = gate_products(j - 1, v - 1)
                 if j + 1 < N_TILES and v < 2:
                     prepare_cat_half(j + 1, v == 0)
-                if v % 2 == 1:
-                    quantise_hidden(j, v // 2, hid)
+                if v % HALVES == 1:
+                    quantise_hidden(j, v // HALVES, hid)
                 if v > 0:
                     gate_apply(j - 1, v - 1, res)
             gate_apply(j - 1, QUARTERS - 1, gate_products(j - 1, QUARTERS - 1))

from contextlib import ExitStack

import concourse.mybir as mybir
from concourse.masks import make_identity

F32 = mybir.dt.float32
BF16 = mybir.dt.bfloat16
U32 = mybir.dt.uint32
U8 = mybir.dt.uint8
FP8X4 = mybir.dt.float8_e4m3fn_x4
ACT = mybir.ActivationFunctionType
ALU = mybir.AluOpType

P = 128
PACK = 4
HALVES = 2
ROWS = 2
QUARTERS = 4
IMAGES = 6
CH = 1024
PIX = 256
HID = 1024
TILE_IMAGES = 2
N_TILE = TILE_IMAGES * PIX
N_TILES = IMAGES // TILE_IMAGES
C_PASSES = 2 * CH // (P * PACK)
X_PASSES = C_PASSES // 2
G_PASSES = HID // (P * PACK)
BANK_PASSES = 2
PSUM_BANKS = 8
RUN = 4

FLOPS = 2 * IMAGES * PIX * (2 * CH * HID + HID * CH)


def tile_graphaugmentation_pb_kernel(tc, x, agg, g1w, g1b, g2w, g2b, out):
    nc = tc.nc

    def by_quarters(images):
        return images.rearrange("b (v p e) h w -> p b v e (h w)", v=QUARTERS, p=P, e=ROWS)

    x_rows = by_quarters(x)
    agg_rows = by_quarters(agg)
    out_rows = by_quarters(out)
    g1w_rows = g1w.rearrange("(v p e) c -> p v e c", v=QUARTERS, p=P, e=ROWS)
    g2w_rows = g2w.rearrange("(v p e) g -> p v e g", v=QUARTERS, p=P, e=ROWS)

    with ExitStack() as ctx:
        keep = ctx.enter_context(tc.tile_pool(name="keep", bufs=1))
        cat_stage = ctx.enter_context(tc.tile_pool(name="cat_stage", bufs=3))
        w_stage = ctx.enter_context(tc.tile_pool(name="w_stage", bufs=4))
        hid_stage = ctx.enter_context(tc.tile_pool(name="hid_stage", bufs=2))
        res_stage = ctx.enter_context(tc.tile_pool(name="res_stage", bufs=5))
        x_stage = ctx.enter_context(tc.tile_pool(name="x_stage", bufs=2))
        psum = ctx.enter_context(tc.psum_pool(name="psum", bufs=PSUM_BANKS))
        ctx.enter_context(tc.manual_schedule())

        ident = keep.tile([P, P], F32, name="ident")
        make_identity(nc, ident[:])

        zero = keep.tile([P, 1], F32, name="zero")
        half = keep.tile([P, 1], F32, name="half")
        nc.vector.memset(zero[:], 0.0)
        nc.scalar.activation(out=half[:], in_=zero[:], func=ACT.Sigmoid)

        b1_bf = keep.tile([P, QUARTERS, ROWS], BF16, name="b1_bf")
        b2_bf = keep.tile([P, QUARTERS, ROWS], BF16, name="b2_bf")

        x_raw = []
        agg_raw = [
            keep.tile([P, TILE_IMAGES, QUARTERS * ROWS, PIX], BF16, name="agg_raw%d" % j)
            for j in range(N_TILES)
        ]
        w1_raw = [keep.tile([P, ROWS, 2 * CH], BF16, name="w1_raw%d" % v) for v in range(QUARTERS)]
        w2_raw = [keep.tile([P, ROWS, HID], BF16, name="w2_raw%d" % v) for v in range(QUARTERS)]

        def load_cat(j):
            x_raw.append(x_stage.tile([P, TILE_IMAGES, QUARTERS * ROWS, PIX], BF16, name="x_raw"))
            for raw, rows in ((x_raw[j], x_rows), (agg_raw[j], agg_rows)):
                for b in range(TILE_IMAGES):
                    nc.sync.dma_start(
                        out=raw[:, b].rearrange("p (v e) w -> p v e w", e=ROWS),
                        in_=rows[:, TILE_IMAGES * j + b],
                    )

        first_quarters = QUARTERS // 2
        load_cat(0)
        for v in range(QUARTERS):
            if v == first_quarters:
                for b_bf, b_dram in ((b1_bf, g1b), (b2_bf, g2b)):
                    nc.sync.dma_start(
                        out=b_bf[:], in_=b_dram.rearrange("(v p e) -> p v e", v=QUARTERS, p=P, e=ROWS)
                    )
            for e in range(ROWS):
                nc.sync.dma_start(out=w1_raw[v][:, e], in_=g1w_rows[:, v, e])
        load_cat(1)
        for v in range(QUARTERS):
            nc.sync.dma_start(out=w2_raw[v][:], in_=g2w_rows[:, v])

        b1 = keep.tile([P, QUARTERS, ROWS], F32, name="b1")
        b2 = keep.tile([P, QUARTERS, ROWS], F32, name="b2")

        cat_codes = [
            keep.tile([P, C_PASSES, N_TILE], U32, name="cat_codes%d" % j, align_bytes=64)
            for j in range(N_TILES)
        ]
        cat_scales = [
            keep.tile([P, C_PASSES, N_TILE], U8, name="cat_scales%d" % j, align_bytes=64)
            for j in range(N_TILES)
        ]
        hid_codes = [
            keep.tile([P, G_PASSES, N_TILE], U32, name="hid_codes%d" % j, align_bytes=64)
            for j in range(N_TILES)
        ]
        hid_scales = [
            keep.tile([P, G_PASSES, N_TILE], U8, name="hid_scales%d" % j, align_bytes=64)
            for j in range(N_TILES)
        ]
        w1_codes = [
            keep.tile([P, ROWS, C_PASSES, P], U32, name="w1_codes%d" % v, align_bytes=64)
            for v in range(QUARTERS)
        ]
        w1_scales = [
            keep.tile([P, ROWS, C_PASSES, P], U8, name="w1_scales%d" % v, align_bytes=64)
            for v in range(QUARTERS)
        ]
        w2_codes = [
            keep.tile([P, ROWS, G_PASSES, P], U32, name="w2_codes%d" % v, align_bytes=64)
            for v in range(QUARTERS)
        ]
        w2_scales = [
            keep.tile([P, ROWS, G_PASSES, P], U8, name="w2_scales%d" % v, align_bytes=64)
            for v in range(QUARTERS)
        ]

        def prepare_cat_half(j, x_half):
            raw = x_raw[j] if x_half else agg_raw[j]
            passes = (0, 1) if x_half else (3, 2)
            tiles = []
            for G in passes:
                first = PACK * (G % X_PASSES)
                grouped = cat_stage.tile([P, N_TILE, PACK], BF16, name="cat_grouped", align_bytes=64)
                dst = grouped[:].rearrange("p (b c i) t -> p b c t i", b=TILE_IMAGES, i=RUN)
                src = raw[:, :, first : first + PACK, :].rearrange("p b t (c i) -> p b c t i", i=RUN)
                if G == C_PASSES - 1:
                    for b in range(TILE_IMAGES):
                        nc.scalar.copy(out=dst[:, b], in_=src[:, b])
                else:
                    nc.vector.tensor_copy(out=dst, in_=src)
                tiles.append(grouped)
            for G, grouped in zip(passes, tiles):
                nc.vector.quantize_mx(
                    out=cat_codes[j][:, G, :].bitcast(FP8X4),
                    scales=cat_scales[j][:, G, :],
                    in_=grouped[:].rearrange("p n t -> p (n t)"),
                )

        def prepare_weights(raw, rows, passes, codes, scales):
            words = raw[:].bitcast(F32)
            grouped = w_stage.tile([P, len(rows), passes, P, PACK], BF16, name="w_grouped", align_bytes=64)
            grouped_words = grouped[:].bitcast(F32)
            for i, e in enumerate(rows):
                for G0 in range(0, passes, BANK_PASSES):
                    bank = psum.tile([P, BANK_PASSES, HALVES, P], F32, name="t_bank", tag="bank")
                    for G in range(G0, G0 + BANK_PASSES):
                        for u in range(HALVES):
                            first = P * (HALVES * G + u)
                            nc.tensor.transpose(
                                out=bank[:, G - G0, u, :],
                                in_=words[:, e, first : first + P],
                                identity=ident[:],
                            )
                    nc.scalar.copy(
                        out=grouped_words[:, i, G0 : G0 + BANK_PASSES, :, :],
                        in_=bank[:].rearrange("p g u m -> p g m u"),
                    )
            these = slice(rows[0], rows[0] + len(rows))
            nc.vector.quantize_mx(
                out=codes[:, these].rearrange("p e g m -> p (e g m)").bitcast(FP8X4),
                scales=scales[:, these].rearrange("p e g m -> p (e g m)"),
                in_=grouped[:].rearrange("p e g m t -> p (e g m t)"),
            )

        def prepare_w1(v):
            for e in range(ROWS):
                prepare_weights(w1_raw[v], (e,), C_PASSES, w1_codes[v], w1_scales[v])

        def prepare_w2(v):
            prepare_weights(w2_raw[v], (0, 1), G_PASSES, w2_codes[v], w2_scales[v])

        def product(w_codes, w_scales, e, passes, rhs_codes, rhs_scales):
            acc = psum.tile([P, N_TILE], F32, name="acc", tag="bank")
            for G in range(passes):
                nc.tensor.matmul_mx(
                    out=acc[:],
                    lhsT=w_codes[:, e, G, :].bitcast(FP8X4),
                    lhsT_scale=w_scales[:, e, G, :],
                    rhs=rhs_codes[:, G, :].bitcast(FP8X4),
                    rhs_scale=rhs_scales[:, G, :],
                    start=(G == 0),
                    stop=(G == passes - 1),
                )
            return acc

        def new_hid():
            return hid_stage.tile([P, PACK, N_TILE], BF16, name="hid")

        def hidden_unit(j, v, e, hid):
            acc = product(w1_codes[v], w1_scales[v], e, C_PASSES, cat_codes[j], cat_scales[j])
            nc.scalar.activation(
                out=hid[:, ROWS * (v % HALVES) + e, :],
                in_=acc[:],
                func=ACT.Relu,
                bias=b1[:, v, e : e + 1],
                scale=1.0,
            )

        def quantise_hidden(j, G, hid):
            grouped = hid_stage.tile([P, N_TILE, PACK], BF16, name="hid_grouped", align_bytes=64)
            nc.vector.tensor_copy(
                out=grouped[:].rearrange("p (c i) t -> p c t i", i=RUN),
                in_=hid[:].rearrange("p t (c i) -> p c t i", i=RUN),
            )
            nc.vector.quantize_mx(
                out=hid_codes[j][:, G, :].bitcast(FP8X4),
                scales=hid_scales[j][:, G, :],
                in_=grouped[:].rearrange("p n t -> p (n t)"),
            )

        def gate_products(j, v):
            res = res_stage.tile([P, TILE_IMAGES, ROWS, PIX], F32, name="res")
            for e in range(ROWS):
                acc = product(w2_codes[v], w2_scales[v], e, G_PASSES, hid_codes[j], hid_scales[j])
                nc.scalar.activation(
                    out=res[:, :, e, :],
                    in_=acc[:].rearrange("p (b w) -> p b w", b=TILE_IMAGES),
                    func=ACT.Sigmoid,
                    bias=b2[:, v, e : e + 1],
                    scale=1.0,
                )
            return res

        def gate_apply(j, v, res):
            nc.vector.tensor_tensor(
                out=res[:], in0=res[:], in1=agg_raw[j][:, :, ROWS * v : ROWS * v + ROWS, :], op=ALU.mult
            )
            nc.sync.dma_start(out=out_rows[:, TILE_IMAGES * j : TILE_IMAGES * j + TILE_IMAGES, v], in_=res[:])

        prepare_cat_half(0, True)
        prepare_cat_half(0, False)
        load_cat(2)
        for v in range(first_quarters):
            prepare_w1(v)
        nc.vector.tensor_copy(out=b1[:], in_=b1_bf[:])
        nc.vector.tensor_copy(out=b2[:], in_=b2_bf[:])

        for v in range(QUARTERS):
            if v % HALVES == 0:
                hid = new_hid()
            for e in range(ROWS):
                hidden_unit(0, v, e, hid)
                if v == 0:
                    prepare_w1(first_quarters + e)
            if v < 2:
                prepare_cat_half(1, v == 0)
            if v == 1:
                quantise_hidden(0, 0, hid)
        prepare_w2(0)
        quantise_hidden(0, 1, hid)
        for v in range(1, QUARTERS):
            prepare_w2(v)

        for j in range(1, N_TILES):
            for v in range(QUARTERS):
                if v % HALVES == 0:
                    hid = new_hid()
                for e in range(ROWS):
                    hidden_unit(j, v, e, hid)
                if v > 0:
                    res = gate_products(j - 1, v - 1)
                if j + 1 < N_TILES and v < 2:
                    prepare_cat_half(j + 1, v == 0)
                if v % HALVES == 1:
                    quantise_hidden(j, v // HALVES, hid)
                if v > 0:
                    gate_apply(j - 1, v - 1, res)
            gate_apply(j - 1, QUARTERS - 1, gate_products(j - 1, QUARTERS - 1))
        for v in range(QUARTERS):
            gate_apply(N_TILES - 1, v, gate_products(N_TILES - 1, v))
